import numpy as np
import ml_dtypes


def mxq(x, axis, fmt="e4m3"):
    dtype, down = {"e4m3": (ml_dtypes.float8_e4m3fn, 7), "e5m2": (ml_dtypes.float8_e5m2, 14)}[fmt]
    v = np.moveaxis(np.asarray(x, np.float32).astype(ml_dtypes.bfloat16).astype(np.float64), axis, -1)
    blocks = v.reshape(v.shape[:-1] + (-1, 32))
    amax = np.abs(blocks).max(-1, keepdims=True)
    byte = np.maximum(np.where(amax > 0, np.frexp(amax)[1] - 1 + 127, 0) - down, 1)
    scale = np.exp2(byte - 127.0)
    codes = (blocks / scale).astype(np.float32).astype(dtype).astype(np.float64)
    return np.moveaxis((codes * scale).reshape(v.shape), -1, axis)


WIDE = False


def mx_kscale(k):
    if not WIDE:
        return np.ones(k)
    levels = np.array([10, -10, 5, -5, 0])
    a = np.random.permutation(np.resize(levels, k // 512 * 4)).reshape(k // 512, 4)
    idx = np.arange(k)
    return np.exp2(a[idx // 512, idx % 128 // 32])


BF16 = ml_dtypes.bfloat16


def bf(x):
    return np.asarray(x, np.float32).astype(BF16)


def f64(x):
    return np.asarray(x).astype(np.float64)


U, I, D = 1024, 4096, 512
C = 1.0
EPS = 1e-7
MAX_SQDIST = 50.0


def setup_inputs():
    s = mx_kscale(D)
    a = np.sqrt(600.0 / np.sqrt(D))
    hu = np.random.standard_normal((U, D)) * a * s
    hi = np.random.standard_normal((I, D)) * a / s
    return {"h": bf(np.concatenate([hu, hi], 0))}


def reference(h):
    h = f64(h)
    hu = h[:U]
    hi = h[U:U + I]
    signs = np.concatenate([-np.ones(1), np.ones(D - 1)])
    prod = mxq(hu, 1, "e4m3") @ mxq(hi * signs, 1, "e4m3").T
    K = 1.0 / C
    theta = np.maximum(-prod / K, 1.0 + EPS)
    sqdist = np.minimum(K * np.arccosh(theta) ** 2, MAX_SQDIST)
    return -sqdist

@@ -1,0 +1,229 @@
+from contextlib import ExitStack
+
+import concourse.mybir as mybir
+from concourse.masks import make_identity
+
+F32 = mybir.dt.float32
+BF16 = mybir.dt.bfloat16
+U32 = mybir.dt.uint32
+U8 = mybir.dt.uint8
+FP8X4 = mybir.dt.float8_e4m3fn_x4
+ALU = mybir.AluOpType
+ACT = mybir.ActivationFunctionType
+
+P = 128
+USERS = 1024
+ITEMS = 4096
+DIM = 512
+FLOPS = 2 * USERS * ITEMS * DIM
+
+PACK = 4
+WORDS = DIM // 2
+USER_TILES = USERS // P
+
+CHUNK_TILES = 4
+CHUNK_ROWS = CHUNK_TILES * P
+ITEM_CHUNKS = ITEMS // CHUNK_ROWS
+BANK_TILES = 2
+
+UNIT_COLS = CHUNK_TILES * CHUNK_ROWS
+HALVES = (slice(0, UNIT_COLS // 2), slice(UNIT_COLS // 2, UNIT_COLS))
+UNITS = (USERS // CHUNK_ROWS) * ITEM_CHUNKS
+BATCH_UNITS = ITEM_CHUNKS
+AHEAD = 2
+
+MIN_THETA = 1.0 + 1e-7
+MAX_SQDIST = 50.0
+EULER = 2.718281828459045
+MAX_THETA = 0.5 * (EULER ** (MAX_SQDIST**0.5) + EULER ** -(MAX_SQDIST**0.5))
+
+
+def tile_hgatmodel_kernel(tc, h, out):
+    nc = tc.nc
+    users = h[0:USERS, :].rearrange("(p t) d -> p t d", t=USER_TILES)
+    out_rows = out.rearrange("(p t) i -> p t i", t=USER_TILES)
+
+    with ExitStack() as ctx:
+        consts = ctx.enter_context(tc.tile_pool(name="consts", bufs=1))
+        operands = ctx.enter_context(tc.tile_pool(name="operands", bufs=1))
+        rows_pool = ctx.enter_context(tc.tile_pool(name="rows", bufs=1))
+        grouped_pool = ctx.enter_context(tc.tile_pool(name="grouped", bufs=2))
+        dist_pool = ctx.enter_context(tc.tile_pool(name="dist", bufs=1))
+        root_pool = ctx.enter_context(tc.tile_pool(name="root", bufs=3))
+        turned_psum = ctx.enter_context(tc.psum_pool(name="turned", bufs=2))
+        prod_psum = ctx.enter_context(tc.psum_pool(name="prod", bufs=6))
+
+        identity = consts.tile([P, P], F32)
+        make_identity(nc, identity[:])
+        one = consts.tile([P, 1], F32)
+        nc.vector.memset(one[:], 1.0)
+        minus_one = consts.tile([P, 1], F32)
+        nc.vector.memset(minus_one[:], -1.0)
+        warm = consts.tile([P, 1], F32)
+        nc.scalar.activation(out=warm[:], in_=one[:], func=ACT.Sqrt)
+
+        user_codes = operands.tile([P, USERS], U32, align_bytes=64)
+        user_scales = operands.tile([P, USERS], U8, align_bytes=64)
+        item_codes = operands.tile([P, ITEMS], U32, align_bytes=64)
+        item_scales = operands.tile([P, ITEMS], U8, align_bytes=64)
+
+        chunks = []
+
+        def add_user_chunk(g):
+            cols = slice(g * CHUNK_ROWS, (g + 1) * CHUNK_ROWS)
+            chunks.append(
+                dict(
+                    source=users[:, g * CHUNK_TILES : (g + 1) * CHUNK_TILES, :],
+                    codes=user_codes[:, cols],
+                    scales=user_scales[:, cols],
+                    is_item=False,
+                )
+            )
+
+        def add_item_chunk(n):
+            cols = slice(n * CHUNK_ROWS, (n + 1) * CHUNK_ROWS)
+            first = USERS + n * CHUNK_ROWS
+            chunks.append(
+                dict(
+                    source=h[first : first + CHUNK_ROWS, :].rearrange("(t p) d -> p t d", p=P),
+                    codes=item_codes[:, cols],
+                    scales=item_scales[:, cols],
+                    is_item=True,
+                )
+            )
+
+        add_user_chunk(0)
+        for n in range(ITEM_CHUNKS):
+            add_item_chunk(n)
+        add_user_chunk(1)
+
+        rows_of = {}
+        grouped_of = {}
+        dist_of = {}
+
+        def load(k):
+            rows_of[k] = rows_pool.tile([P, CHUNK_TILES, DIM], BF16, name="rows%d" % k)
+            nc.sync.dma_start(out=rows_of[k][:], in_=chunks[k]["source"])
+
+        def turn(k):
+            rows = rows_of[k]
+            if chunks[k]["is_item"]:
+                nc.gpsimd.tensor_scalar(
+                    out=rows[:, :, 0:1],
+                    in0=rows[:, :, 0:1],
+                    scalar1=-1.0,
+                    scalar2=0.0,
+                    op0=ALU.mult,
+                    op1=ALU.add,
+                )
+            words = rows[:].rearrange("p t d -> p (t d)").bitcast(F32)
+            grouped = grouped_pool.tile([P, CHUNK_ROWS * PACK], BF16, align_bytes=64)
+            grouped_words = grouped[:].bitcast(F32)
+            bank_words = BANK_TILES * WORDS
+            for b in range(CHUNK_TILES // BANK_TILES):
+                turned = turned_psum.tile([P, BANK_TILES, 2, P], F32)
+                for a in range(BANK_TILES):
+                    for u in range(2):
+                        first = (b * BANK_TILES + a) * WORDS + u * P
+                        nc.tensor.transpose(
+                            out=turned[:, a, u, :],
+                            in_=words[:, first : first + P],
+                            identity=identity[:],
+                        )
+                nc.scalar.copy(
+                    out=grouped_words[:, b * bank_words : (b + 1) * bank_words].rearrange(
+                        "p (a r u) -> p a r u", a=BANK_TILES, u=2
+                    ),
+                    in_=turned[:].rearrange("p a u r -> p a r u"),
+                )
+            grouped_of[k] = grouped
+
+        def quantise(k):
+            nc.vector.quantize_mx(
+                out=chunks[k]["codes"].bitcast(FP8X4),
+                scales=chunks[k]["scales"],
+                in_=grouped_of[k][:],
+            )
+
+        def products(unit):
+            g, n = divmod(unit, ITEM_CHUNKS)
+            item_cols = slice(n * CHUNK_ROWS, (n + 1) * CHUNK_ROWS)
+            dist = dist_pool.tile([P, UNIT_COLS], F32, name="dist%d" % unit)
+            for j in range(CHUNK_TILES):
+                user_cols = slice((g * CHUNK_TILES + j) * P, (g * CHUNK_TILES + j + 1) * P)
+                prod = prod_psum.tile([P, CHUNK_ROWS], F32)
+                nc.tensor.matmul_mx(
+                    out=prod[:],
+                    lhsT=user_codes[:, user_cols].bitcast(FP8X4),
+                    lhsT_scale=user_scales[:, user_cols],
+                    rhs=item_codes[:, item_cols].bitcast(FP8X4),
+                    rhs_scale=item_scales[:, item_cols],
+                    start=True,
+                    stop=True,
+                )
+                nc.vector.tensor_scalar(
+                    out=dist[:, j * CHUNK_ROWS : (j + 1) * CHUNK_ROWS],
+                    in0=prod[:],
+                    scalar1=-MIN_THETA,
+                    scalar2=-MAX_THETA,
+                    op0=ALU.min,
+                    op1=ALU.max,
+                )
+            dist_of[unit] = dist
+
+        def roots(unit):
+            dist = dist_of[unit]
+            root = root_pool.tile([P, UNIT_COLS], F32)
+            for half in HALVES:
+                nc.scalar.activation(out=root[:, half], in_=dist[:, half], func=ACT.Square)
+            for half in HALVES:
+                nc.scalar.activation(
+                    out=root[:, half], in_=root[:, half], func=ACT.Sqrt, bias=minus_one[:]
+                )
+            for half in HALVES:
+                nc.vector.tensor_tensor(
+                    out=dist[:, half], in0=root[:, half], in1=dist[:, half], op=ALU.subtract
+                )
+
+        def logs(unit):
+            g, n = divmod(unit, ITEM_CHUNKS)
+            dist = dist_of[unit]
+            for half in HALVES:
+                nc.scalar.activation(out=dist[:, half], in_=dist[:, half], func=ACT.Ln)
+            for half in HALVES:
+                nc.vector.scalar_tensor_tensor(
+                    out=dist[:, half],
+                    in0=dist[:, half],
+                    scalar=-1.0,
+                    in1=dist[:, half],
+                    op0=ALU.mult,
+                    op1=ALU.mult,
+                )
+            nc.sync.dma_start(
+                out=out_rows[
+                    :,
+                    g * CHUNK_TILES : (g + 1) * CHUNK_TILES,
+                    n * CHUNK_ROWS : (n + 1) * CHUNK_ROWS,
+                ],
+                in_=dist[:].rearrange("p (j c) -> p j c", j=CHUNK_TILES),
+            )
+
+        with tc.manual_schedule():
+            for k in range(len(chunks)):
+                load(k)
+            turn(0)
+            turn(1)
+            quantise(0)
+            for u in range(UNITS + AHEAD):
+                behind = u - AHEAD
+                if behind >= 0:
+                    roots(behind)
+                    if behind % BATCH_UNITS == BATCH_UNITS - 1:
+                        for unit in range(behind + 1 - BATCH_UNITS, behind + 1):
+                            logs(unit)
+                if u + 2 < len(chunks):
+                    turn(u + 2)
+                if u + 1 < len(chunks):
+                    quantise(u + 1)
+                if u < UNITS:
+                    products(u)

@@ -27,10 +27,13 @@ ITEM_CHUNKS = ITEMS // CHUNK_ROWS
 BANK_TILES = 2
 
 UNIT_COLS = CHUNK_TILES * CHUNK_ROWS
-HALVES = (slice(0, UNIT_COLS // 2), slice(UNIT_COLS // 2, UNIT_COLS))
 UNITS = (USERS // CHUNK_ROWS) * ITEM_CHUNKS
+PIECE_TILES = 2
+PIECE_COLS = PIECE_TILES * CHUNK_ROWS
 BATCH_UNITS = ITEM_CHUNKS
-AHEAD = 2
+SQUARE_LAG = 2
+ROOT_LAG = 3
+SUM_LAG = 4
 
 MIN_THETA = 1.0 + 1e-7
 MAX_SQDIST = 50.0
@@ -46,10 +49,10 @@ def tile_hgatmodel_kernel(tc, h, out):
     with ExitStack() as ctx:
         consts = ctx.enter_context(tc.tile_pool(name="consts", bufs=1))
         operands = ctx.enter_context(tc.tile_pool(name="operands", bufs=1))
-        rows_pool = ctx.enter_context(tc.tile_pool(name="rows", bufs=1))
+        rows_pool = ctx.enter_context(tc.tile_pool(name="rows", bufs=6))
         grouped_pool = ctx.enter_context(tc.tile_pool(name="grouped", bufs=2))
         dist_pool = ctx.enter_context(tc.tile_pool(name="dist", bufs=1))
-        root_pool = ctx.enter_context(tc.tile_pool(name="root", bufs=3))
+        root_pool = ctx.enter_context(tc.tile_pool(name="root", bufs=4))
         turned_psum = ctx.enter_context(tc.psum_pool(name="turned", bufs=2))
         prod_psum = ctx.enter_context(tc.psum_pool(name="prod", bufs=6))
 
@@ -100,10 +103,12 @@ def tile_hgatmodel_kernel(tc, h, out):
         rows_of = {}
         grouped_of = {}
         dist_of = {}
+        root_of = {}
 
         def load(k):
-            rows_of[k] = rows_pool.tile([P, CHUNK_TILES, DIM], BF16, name="rows%d" % k)
-            nc.sync.dma_start(out=rows_of[k][:], in_=chunks[k]["source"])
+            rows = rows_pool.tile([P, CHUNK_TILES, DIM], BF16)
+            nc.sync.dma_start(out=rows[:], in_=chunks[k]["source"])
+            rows_of[k] = rows
 
         def turn(k):
             rows = rows_of[k]
@@ -130,12 +135,15 @@ def tile_hgatmodel_kernel(tc, h, out):
                             in_=words[:, first : first + P],
                             identity=identity[:],
                         )
-                nc.scalar.copy(
-                    out=grouped_words[:, b * bank_words : (b + 1) * bank_words].rearrange(
-                        "p (a r u) -> p a r u", a=BANK_TILES, u=2
-                    ),
-                    in_=turned[:].rearrange("p a u r -> p a r u"),
+                side_by_side = grouped_words[:, b * bank_words : (b + 1) * bank_words].rearrange(
+                    "p (a r u) -> p a r u", a=BANK_TILES, u=2
                 )
+                if b == 0:
+                    nc.vector.tensor_copy(
+                        out=side_by_side, in_=turned[:].rearrange("p a u r -> p a r u")
+                    )
+                else:
+                    nc.scalar.copy(out=side_by_side, in_=turned[:].rearrange("p a u r -> p a r u"))
             grouped_of[k] = grouped
 
         def quantise(k):
@@ -171,42 +179,44 @@ def tile_hgatmodel_kernel(tc, h, out):
                 )
             dist_of[unit] = dist
 
-        def roots(unit):
-            dist = dist_of[unit]
+        def squares(unit):
             root = root_pool.tile([P, UNIT_COLS], F32)
-            for half in HALVES:
-                nc.scalar.activation(out=root[:, half], in_=dist[:, half], func=ACT.Square)
-            for half in HALVES:
-                nc.scalar.activation(
-                    out=root[:, half], in_=root[:, half], func=ACT.Sqrt, bias=minus_one[:]
-                )
-            for half in HALVES:
-                nc.vector.tensor_tensor(
-                    out=dist[:, half], in0=root[:, half], in1=dist[:, half], op=ALU.subtract
-                )
+            nc.scalar.activation(out=root[:], in_=dist_of[unit][:], func=ACT.Square)
+            root_of[unit] = root
+
+        def roots(unit):
+            root = root_of[unit]
+            nc.scalar.activation(out=root[:], in_=root[:], func=ACT.Sqrt, bias=minus_one[:])
+
+        def sums(unit):
+            dist = dist_of[unit]
+            nc.vector.tensor_tensor(
+                out=dist[:], in0=root_of[unit][:], in1=dist[:], op=ALU.subtract
+            )
 
         def logs(unit):
             g, n = divmod(unit, ITEM_CHUNKS)
             dist = dist_of[unit]
-            for half in HALVES:
-                nc.scalar.activation(out=dist[:, half], in_=dist[:, half], func=ACT.Ln)
-            for half in HALVES:
+            for piece in range(CHUNK_TILES // PIECE_TILES):
+                cols = slice(piece * PIECE_COLS, (piece + 1) * PIECE_COLS)
+                first_tile = g * CHUNK_TILES + piece * PIECE_TILES
+                nc.scalar.activation(out=dist[:, cols], in_=dist[:, cols], func=ACT.Ln)
                 nc.vector.scalar_tensor_tensor(
-                    out=dist[:, half],
-                    in0=dist[:, half],
+                    out=dist[:, cols],
+                    in0=dist[:, cols],
                     scalar=-1.0,
-                    in1=dist[:, half],
+                    in1=dist[:, cols],
                     op0=ALU.mult,
                     op1=ALU.mult,
                 )
-            nc.sync.dma_start(
-                out=out_rows[
-                    :,
-                    g * CHUNK_TILES : (g + 1) * CHUNK_TILES,
-                    n * CHUNK_ROWS : (n + 1) * CHUNK_ROWS,
-                ],
-                in_=dist[:].rearrange("p (j c) -> p j c", j=CHUNK_TILES),
-            )
+                nc.sync.dma_start(
+                    out=out_rows[
+                        :,
+                        first_tile : first_tile + PIECE_TILES,
+                        n * CHUNK_ROWS : (n + 1) * CHUNK_ROWS,
+                    ],
+                    in_=dist[:, cols].rearrange("p (j c) -> p j c", j=PIECE_TILES),
+                )
 
         with tc.manual_schedule():
             for k in range(len(chunks)):
@@ -214,16 +224,20 @@ def tile_hgatmodel_kernel(tc, h, out):
             turn(0)
             turn(1)
             quantise(0)
-            for u in range(UNITS + AHEAD):
-                behind = u - AHEAD
-                if behind >= 0:
-                    roots(behind)
-                    if behind % BATCH_UNITS == BATCH_UNITS - 1:
-                        for unit in range(behind + 1 - BATCH_UNITS, behind + 1):
+            for r in range(UNITS + SUM_LAG):
+                if 0 <= r - SQUARE_LAG < UNITS:
+                    squares(r - SQUARE_LAG)
+                if 0 <= r - ROOT_LAG < UNITS:
+                    roots(r - ROOT_LAG)
+                summed = r - SUM_LAG
+                if summed >= 0:
+                    sums(summed)
+                    if summed % BATCH_UNITS == BATCH_UNITS - 1:
+                        for unit in range(summed + 1 - BATCH_UNITS, summed + 1):
                             logs(unit)
-                if u + 2 < len(chunks):
-                    turn(u + 2)
-                if u + 1 < len(chunks):
-                    quantise(u + 1)
-                if u < UNITS:
-                    products(u)
+                if r + 1 < len(chunks):
+                    quantise(r + 1)
+                if r < UNITS:
+                    products(r)
+                if r + 2 < len(chunks):
+                    turn(r + 2)

@@ -23,16 +23,19 @@ USER_TILES = USERS // P
 
 CHUNK_TILES = 4
 CHUNK_ROWS = CHUNK_TILES * P
+USER_CHUNKS = USERS // CHUNK_ROWS
 ITEM_CHUNKS = ITEMS // CHUNK_ROWS
 BANK_TILES = 2
 
-UNIT_COLS = CHUNK_TILES * CHUNK_ROWS
-UNITS = (USERS // CHUNK_ROWS) * ITEM_CHUNKS
-PIECE_TILES = 2
-PIECE_COLS = PIECE_TILES * CHUNK_ROWS
-BATCH_UNITS = ITEM_CHUNKS
-SQUARE_LAG = 2
-ROOT_LAG = 3
+UNITS = USER_CHUNKS * ITEM_CHUNKS
+POOL_TILES = 1
+MAIN_TILES = CHUNK_TILES - POOL_TILES
+LOG_COLS = 1024
+
+TURN_LEAD = 2
+QUANTISE_LEAD = 1
+SQUARE_LAG = 1
+ROOT_LAG = 2
 SUM_LAG = 4
 
 MIN_THETA = 1.0 + 1e-7
@@ -60,8 +63,6 @@ def tile_hgatmodel_kernel(tc, h, out):
         make_identity(nc, identity[:])
         one = consts.tile([P, 1], F32)
         nc.vector.memset(one[:], 1.0)
-        minus_one = consts.tile([P, 1], F32)
-        nc.vector.memset(minus_one[:], -1.0)
         warm = consts.tile([P, 1], F32)
         nc.scalar.activation(out=warm[:], in_=one[:], func=ACT.Sqrt)
 
@@ -70,49 +71,41 @@ def tile_hgatmodel_kernel(tc, h, out):
         item_codes = operands.tile([P, ITEMS], U32, align_bytes=64)
         item_scales = operands.tile([P, ITEMS], U8, align_bytes=64)
 
-        chunks = []
+        dist = dist_pool.tile([P, USER_TILES, ITEMS], F32)
 
-        def add_user_chunk(g):
+        def user_chunk(g):
             cols = slice(g * CHUNK_ROWS, (g + 1) * CHUNK_ROWS)
-            chunks.append(
-                dict(
-                    source=users[:, g * CHUNK_TILES : (g + 1) * CHUNK_TILES, :],
-                    codes=user_codes[:, cols],
-                    scales=user_scales[:, cols],
-                    is_item=False,
-                )
+            return dict(
+                source=users[:, g * CHUNK_TILES : (g + 1) * CHUNK_TILES, :],
+                codes=user_codes[:, cols],
+                scales=user_scales[:, cols],
+                is_item=False,
             )
 
-        def add_item_chunk(n):
+        def item_chunk(n):
             cols = slice(n * CHUNK_ROWS, (n + 1) * CHUNK_ROWS)
             first = USERS + n * CHUNK_ROWS
-            chunks.append(
-                dict(
-                    source=h[first : first + CHUNK_ROWS, :].rearrange("(t p) d -> p t d", p=P),
-                    codes=item_codes[:, cols],
-                    scales=item_scales[:, cols],
-                    is_item=True,
-                )
+            return dict(
+                source=h[first : first + CHUNK_ROWS, :].rearrange("(t p) d -> p t d", p=P),
+                codes=item_codes[:, cols],
+                scales=item_scales[:, cols],
+                is_item=True,
+                first_round=USER_CHUNKS * n,
             )
 
-        add_user_chunk(0)
-        for n in range(ITEM_CHUNKS):
-            add_item_chunk(n)
-        add_user_chunk(1)
+        first_chunks = [user_chunk(g) for g in range(USER_CHUNKS)] + [item_chunk(0)]
+        later_chunks = [item_chunk(n) for n in range(1, ITEM_CHUNKS)]
 
-        rows_of = {}
-        grouped_of = {}
-        dist_of = {}
         root_of = {}
 
-        def load(k):
+        def load(chunk):
             rows = rows_pool.tile([P, CHUNK_TILES, DIM], BF16)
-            nc.sync.dma_start(out=rows[:], in_=chunks[k]["source"])
-            rows_of[k] = rows
+            nc.sync.dma_start(out=rows[:], in_=chunk["source"])
+            chunk["rows"] = rows
 
-        def turn(k):
-            rows = rows_of[k]
-            if chunks[k]["is_item"]:
+        def turn(chunk):
+            rows = chunk["rows"]
+            if chunk["is_item"]:
                 nc.gpsimd.tensor_scalar(
                     out=rows[:, :, 0:1],
                     in0=rows[:, :, 0:1],
@@ -135,30 +128,33 @@ def tile_hgatmodel_kernel(tc, h, out):
                             in_=words[:, first : first + P],
                             identity=identity[:],
                         )
-                side_by_side = grouped_words[:, b * bank_words : (b + 1) * bank_words].rearrange(
-                    "p (a r u) -> p a r u", a=BANK_TILES, u=2
+                nc.scalar.copy(
+                    out=grouped_words[:, b * bank_words : (b + 1) * bank_words].rearrange(
+                        "p (a r u) -> p a r u", a=BANK_TILES, u=2
+                    ),
+                    in_=turned[:].rearrange("p a u r -> p a r u"),
                 )
-                if b == 0:
-                    nc.vector.tensor_copy(
-                        out=side_by_side, in_=turned[:].rearrange("p a u r -> p a r u")
-                    )
-                else:
-                    nc.scalar.copy(out=side_by_side, in_=turned[:].rearrange("p a u r -> p a r u"))
-            grouped_of[k] = grouped
+            chunk["grouped"] = grouped
 
-        def quantise(k):
+        def quantise(chunk):
             nc.vector.quantize_mx(
-                out=chunks[k]["codes"].bitcast(FP8X4),
-                scales=chunks[k]["scales"],
-                in_=grouped_of[k][:],
+                out=chunk["codes"].bitcast(FP8X4),
+                scales=chunk["scales"],
+                in_=chunk["grouped"][:],
             )
 
+        def part_of_dist(unit):
+            n, g = divmod(unit, USER_CHUNKS)
+            return dist[
+                :, g * CHUNK_TILES : (g + 1) * CHUNK_TILES, n * CHUNK_ROWS : (n + 1) * CHUNK_ROWS
+            ]
+
         def products(unit):
-            g, n = divmod(unit, ITEM_CHUNKS)
+            n, g = divmod(unit, USER_CHUNKS)
             item_cols = slice(n * CHUNK_ROWS, (n + 1) * CHUNK_ROWS)
-            dist = dist_pool.tile([P, UNIT_COLS], F32, name="dist%d" % unit)
             for j in range(CHUNK_TILES):
-                user_cols = slice((g * CHUNK_TILES + j) * P, (g * CHUNK_TILES + j + 1) * P)
+                user_tile = g * CHUNK_TILES + j
+                user_cols = slice(user_tile * P, (user_tile + 1) * P)
                 prod = prod_psum.tile([P, CHUNK_ROWS], F32)
                 nc.tensor.matmul_mx(
                     out=prod[:],
@@ -170,74 +166,79 @@ def tile_hgatmodel_kernel(tc, h, out):
                     stop=True,
                 )
                 nc.vector.tensor_scalar(
-                    out=dist[:, j * CHUNK_ROWS : (j + 1) * CHUNK_ROWS],
+                    out=dist[:, user_tile, item_cols],
                     in0=prod[:],
                     scalar1=-MIN_THETA,
                     scalar2=-MAX_THETA,
                     op0=ALU.min,
                     op1=ALU.max,
                 )
-            dist_of[unit] = dist
 
         def squares(unit):
-            root = root_pool.tile([P, UNIT_COLS], F32)
-            nc.scalar.activation(out=root[:], in_=dist_of[unit][:], func=ACT.Square)
+            root = root_pool.tile([P, CHUNK_TILES, CHUNK_ROWS], F32)
+            part = part_of_dist(unit)
+            nc.gpsimd.tensor_tensor(
+                out=root[:, MAIN_TILES:, :],
+                in0=part[:, MAIN_TILES:, :],
+                in1=part[:, MAIN_TILES:, :],
+                op=ALU.mult,
+            )
+            nc.scalar.activation(
+                out=root[:, :MAIN_TILES, :], in_=part[:, :MAIN_TILES, :], func=ACT.Square
+            )
             root_of[unit] = root
 
         def roots(unit):
             root = root_of[unit]
-            nc.scalar.activation(out=root[:], in_=root[:], func=ACT.Sqrt, bias=minus_one[:])
+            nc.scalar.activation(out=root[:], in_=root[:], func=ACT.Sqrt, bias=-1.0)
 
         def sums(unit):
-            dist = dist_of[unit]
+            root = root_of[unit]
+            part = part_of_dist(unit)
+            nc.gpsimd.tensor_tensor(
+                out=part[:, MAIN_TILES:, :],
+                in0=root[:, MAIN_TILES:, :],
+                in1=part[:, MAIN_TILES:, :],
+                op=ALU.subtract,
+            )
             nc.vector.tensor_tensor(
-                out=dist[:], in0=root_of[unit][:], in1=dist[:], op=ALU.subtract
+                out=part[:, :MAIN_TILES, :],
+                in0=root[:, :MAIN_TILES, :],
+                in1=part[:, :MAIN_TILES, :],
+                op=ALU.subtract,
             )
 
-        def logs(unit):
-            g, n = divmod(unit, ITEM_CHUNKS)
-            dist = dist_of[unit]
-            for piece in range(CHUNK_TILES // PIECE_TILES):
-                cols = slice(piece * PIECE_COLS, (piece + 1) * PIECE_COLS)
-                first_tile = g * CHUNK_TILES + piece * PIECE_TILES
-                nc.scalar.activation(out=dist[:, cols], in_=dist[:, cols], func=ACT.Ln)
-                nc.vector.scalar_tensor_tensor(
-                    out=dist[:, cols],
-                    in0=dist[:, cols],
-                    scalar=-1.0,
-                    in1=dist[:, cols],
-                    op0=ALU.mult,
-                    op1=ALU.mult,
-                )
-                nc.sync.dma_start(
-                    out=out_rows[
-                        :,
-                        first_tile : first_tile + PIECE_TILES,
-                        n * CHUNK_ROWS : (n + 1) * CHUNK_ROWS,
-                    ],
-                    in_=dist[:, cols].rearrange("p (j c) -> p j c", j=PIECE_TILES),
-                )
+        def logs():
+            for first in range(0, ITEMS, LOG_COLS):
+                for user_tile in range(USER_TILES):
+                    piece = dist[:, user_tile, first : first + LOG_COLS]
+                    nc.scalar.activation(out=piece, in_=piece, func=ACT.Ln)
+                    nc.vector.scalar_tensor_tensor(
+                        out=piece, in0=piece, scalar=-1.0, in1=piece, op0=ALU.mult, op1=ALU.mult
+                    )
+                    nc.sync.dma_start(
+                        out=out_rows[:, user_tile, first : first + LOG_COLS], in_=piece
+                    )
 
         with tc.manual_schedule():
-            for k in range(len(chunks)):
-                load(k)
-            turn(0)
-            turn(1)
-            quantise(0)
+            for chunk in first_chunks + later_chunks:
+                load(chunk)
+            for chunk in first_chunks:
+                turn(chunk)
+                quantise(chunk)
             for r in range(UNITS + SUM_LAG):
                 if 0 <= r - SQUARE_LAG < UNITS:
                     squares(r - SQUARE_LAG)
                 if 0 <= r - ROOT_LAG < UNITS:
                     roots(r - ROOT_LAG)
-                summed = r - SUM_LAG
-                if summed >= 0:
-                    sums(summed)
-                    if summed % BATCH_UNITS == BATCH_UNITS - 1:
-                        for unit in range(summed + 1 - BATCH_UNITS, summed + 1):
-                            logs(unit)
-                if r + 1 < len(chunks):
-                    quantise(r + 1)
+                if 0 <= r - SUM_LAG:
+                    sums(r - SUM_LAG)
                 if r < UNITS:
                     products(r)
-                if r + 2 < len(chunks):
-                    turn(r + 2)
+                for chunk in later_chunks:
+                    if chunk["first_round"] == r + QUANTISE_LEAD:
+                        quantise(chunk)
+                for chunk in later_chunks:
+                    if chunk["first_round"] == r + TURN_LEAD:
+                        turn(chunk)
+            logs()

@@ -28,8 +28,8 @@ ITEM_CHUNKS = ITEMS // CHUNK_ROWS
 BANK_TILES = 2
 
 UNITS = USER_CHUNKS * ITEM_CHUNKS
-POOL_TILES = 1
-MAIN_TILES = CHUNK_TILES - POOL_TILES
+POOL_COLS = 96
+MAIN_COLS = CHUNK_ROWS - POOL_COLS
 LOG_COLS = 1024
 
 TURN_LEAD = 2
@@ -100,20 +100,15 @@ def tile_hgatmodel_kernel(tc, h, out):
 
         def load(chunk):
             rows = rows_pool.tile([P, CHUNK_TILES, DIM], BF16)
-            nc.sync.dma_start(out=rows[:], in_=chunk["source"])
+            for first in range(0, CHUNK_TILES, BANK_TILES):
+                tiles = slice(first, first + BANK_TILES)
+                nc.sync.dma_start(out=rows[:, tiles, :], in_=chunk["source"][:, tiles, :])
             chunk["rows"] = rows
 
         def turn(chunk):
             rows = chunk["rows"]
             if chunk["is_item"]:
-                nc.gpsimd.tensor_scalar(
-                    out=rows[:, :, 0:1],
-                    in0=rows[:, :, 0:1],
-                    scalar1=-1.0,
-                    scalar2=0.0,
-                    op0=ALU.mult,
-                    op1=ALU.add,
-                )
+                nc.vector.tensor_scalar_mul(out=rows[:, :, 0:1], in0=rows[:, :, 0:1], scalar1=-1.0)
             words = rows[:].rearrange("p t d -> p (t d)").bitcast(F32)
             grouped = grouped_pool.tile([P, CHUNK_ROWS * PACK], BF16, align_bytes=64)
             grouped_words = grouped[:].bitcast(F32)
@@ -178,13 +173,13 @@ def tile_hgatmodel_kernel(tc, h, out):
             root = root_pool.tile([P, CHUNK_TILES, CHUNK_ROWS], F32)
             part = part_of_dist(unit)
             nc.gpsimd.tensor_tensor(
-                out=root[:, MAIN_TILES:, :],
-                in0=part[:, MAIN_TILES:, :],
-                in1=part[:, MAIN_TILES:, :],
+                out=root[:, :, MAIN_COLS:],
+                in0=part[:, :, MAIN_COLS:],
+                in1=part[:, :, MAIN_COLS:],
                 op=ALU.mult,
             )
             nc.scalar.activation(
-                out=root[:, :MAIN_TILES, :], in_=part[:, :MAIN_TILES, :], func=ACT.Square
+                out=root[:, :, :MAIN_COLS], in_=part[:, :, :MAIN_COLS], func=ACT.Square
             )
             root_of[unit] = root
 
@@ -196,15 +191,15 @@ def tile_hgatmodel_kernel(tc, h, out):
             root = root_of[unit]
             part = part_of_dist(unit)
             nc.gpsimd.tensor_tensor(
-                out=part[:, MAIN_TILES:, :],
-                in0=root[:, MAIN_TILES:, :],
-                in1=part[:, MAIN_TILES:, :],
+                out=part[:, :, MAIN_COLS:],
+                in0=root[:, :, MAIN_COLS:],
+                in1=part[:, :, MAIN_COLS:],
                 op=ALU.subtract,
             )
             nc.vector.tensor_tensor(
-                out=part[:, :MAIN_TILES, :],
-                in0=root[:, :MAIN_TILES, :],
-                in1=part[:, :MAIN_TILES, :],
+                out=part[:, :, :MAIN_COLS],
+                in0=root[:, :, :MAIN_COLS],
+                in1=part[:, :, :MAIN_COLS],
                 op=ALU.subtract,
             )
 

@@ -23,17 +23,18 @@ USER_TILES = USERS // P
 
 CHUNK_TILES = 4
 CHUNK_ROWS = CHUNK_TILES * P
-USER_CHUNKS = USERS // CHUNK_ROWS
 ITEM_CHUNKS = ITEMS // CHUNK_ROWS
 BANK_TILES = 2
 
-UNITS = USER_CHUNKS * ITEM_CHUNKS
-POOL_COLS = 96
-MAIN_COLS = CHUNK_ROWS - POOL_COLS
-LOG_COLS = 1024
+UNIT_TILES = 2
+UNIT_CHUNKS = 2
+ROW_COLS = UNIT_CHUNKS * CHUNK_ROWS
+UNIT_COLS = UNIT_TILES * ROW_COLS
+USER_PAIRS = USER_TILES // UNIT_TILES
+UNITS = USER_PAIRS * (ITEM_CHUNKS // UNIT_CHUNKS)
+POOL_COLS = 384
+MAIN_COLS = UNIT_COLS - POOL_COLS
 
-TURN_LEAD = 2
-QUANTISE_LEAD = 1
 SQUARE_LAG = 1
 ROOT_LAG = 2
 SUM_LAG = 4
@@ -71,8 +72,6 @@ def tile_hgatmodel_kernel(tc, h, out):
         item_codes = operands.tile([P, ITEMS], U32, align_bytes=64)
         item_scales = operands.tile([P, ITEMS], U8, align_bytes=64)
 
-        dist = dist_pool.tile([P, USER_TILES, ITEMS], F32)
-
         def user_chunk(g):
             cols = slice(g * CHUNK_ROWS, (g + 1) * CHUNK_ROWS)
             return dict(
@@ -90,12 +89,12 @@ def tile_hgatmodel_kernel(tc, h, out):
                 codes=item_codes[:, cols],
                 scales=item_scales[:, cols],
                 is_item=True,
-                first_round=USER_CHUNKS * n,
             )
 
-        first_chunks = [user_chunk(g) for g in range(USER_CHUNKS)] + [item_chunk(0)]
-        later_chunks = [item_chunk(n) for n in range(1, ITEM_CHUNKS)]
+        first_chunks = [user_chunk(0), item_chunk(0), item_chunk(1)]
+        later_chunks = [user_chunk(1)] + [item_chunk(n) for n in range(UNIT_CHUNKS, ITEM_CHUNKS)]
 
+        dist_of = {}
         root_of = {}
 
         def load(chunk):
@@ -105,10 +104,13 @@ def tile_hgatmodel_kernel(tc, h, out):
                 nc.sync.dma_start(out=rows[:, tiles, :], in_=chunk["source"][:, tiles, :])
             chunk["rows"] = rows
 
+        def flip_sign(chunk):
+            if chunk["is_item"]:
+                first_coordinate = chunk["rows"][:, :, 0:1]
+                nc.vector.tensor_scalar_mul(out=first_coordinate, in0=first_coordinate, scalar1=-1.0)
+
         def turn(chunk):
             rows = chunk["rows"]
-            if chunk["is_item"]:
-                nc.vector.tensor_scalar_mul(out=rows[:, :, 0:1], in0=rows[:, :, 0:1], scalar1=-1.0)
             words = rows[:].rearrange("p t d -> p (t d)").bitcast(F32)
             grouped = grouped_pool.tile([P, CHUNK_ROWS * PACK], BF16, align_bytes=64)
             grouped_words = grouped[:].bitcast(F32)
@@ -138,48 +140,40 @@ def tile_hgatmodel_kernel(tc, h, out):
                 in_=chunk["grouped"][:],
             )
 
-        def part_of_dist(unit):
-            n, g = divmod(unit, USER_CHUNKS)
-            return dist[
-                :, g * CHUNK_TILES : (g + 1) * CHUNK_TILES, n * CHUNK_ROWS : (n + 1) * CHUNK_ROWS
-            ]
-
         def products(unit):
-            n, g = divmod(unit, USER_CHUNKS)
-            item_cols = slice(n * CHUNK_ROWS, (n + 1) * CHUNK_ROWS)
-            for j in range(CHUNK_TILES):
-                user_tile = g * CHUNK_TILES + j
-                user_cols = slice(user_tile * P, (user_tile + 1) * P)
-                prod = prod_psum.tile([P, CHUNK_ROWS], F32)
-                nc.tensor.matmul_mx(
-                    out=prod[:],
-                    lhsT=user_codes[:, user_cols].bitcast(FP8X4),
-                    lhsT_scale=user_scales[:, user_cols],
-                    rhs=item_codes[:, item_cols].bitcast(FP8X4),
-                    rhs_scale=item_scales[:, item_cols],
-                    start=True,
-                    stop=True,
-                )
-                nc.vector.tensor_scalar(
-                    out=dist[:, user_tile, item_cols],
-                    in0=prod[:],
-                    scalar1=-MIN_THETA,
-                    scalar2=-MAX_THETA,
-                    op0=ALU.min,
-                    op1=ALU.max,
-                )
+            m, q = divmod(unit, USER_PAIRS)
+            dist = dist_pool.tile([P, UNIT_COLS], F32, name="dist%d" % unit)
+            for j in range(UNIT_TILES):
+                user_first = (q * UNIT_TILES + j) * P
+                for c in range(UNIT_CHUNKS):
+                    item_first = (m * UNIT_CHUNKS + c) * CHUNK_ROWS
+                    prod = prod_psum.tile([P, CHUNK_ROWS], F32)
+                    nc.tensor.matmul_mx(
+                        out=prod[:],
+                        lhsT=user_codes[:, user_first : user_first + P].bitcast(FP8X4),
+                        lhsT_scale=user_scales[:, user_first : user_first + P],
+                        rhs=item_codes[:, item_first : item_first + CHUNK_ROWS].bitcast(FP8X4),
+                        rhs_scale=item_scales[:, item_first : item_first + CHUNK_ROWS],
+                        start=True,
+                        stop=True,
+                    )
+                    dist_first = j * ROW_COLS + c * CHUNK_ROWS
+                    nc.vector.tensor_scalar(
+                        out=dist[:, dist_first : dist_first + CHUNK_ROWS],
+                        in0=prod[:],
+                        scalar1=-MIN_THETA,
+                        scalar2=-MAX_THETA,
+                        op0=ALU.min,
+                        op1=ALU.max,
+                    )
+            dist_of[unit] = dist
 
         def squares(unit):
-            root = root_pool.tile([P, CHUNK_TILES, CHUNK_ROWS], F32)
-            part = part_of_dist(unit)
+            dist = dist_of[unit]
+            root = root_pool.tile([P, UNIT_COLS], F32)
+            nc.scalar.activation(out=root[:, :MAIN_COLS], in_=dist[:, :MAIN_COLS], func=ACT.Square)
             nc.gpsimd.tensor_tensor(
-                out=root[:, :, MAIN_COLS:],
-                in0=part[:, :, MAIN_COLS:],
-                in1=part[:, :, MAIN_COLS:],
-                op=ALU.mult,
-            )
-            nc.scalar.activation(
-                out=root[:, :, :MAIN_COLS], in_=part[:, :, :MAIN_COLS], func=ACT.Square
+                out=root[:, MAIN_COLS:], in0=dist[:, MAIN_COLS:], in1=dist[:, MAIN_COLS:], op=ALU.mult
             )
             root_of[unit] = root
 
@@ -188,36 +182,32 @@ def tile_hgatmodel_kernel(tc, h, out):
             nc.scalar.activation(out=root[:], in_=root[:], func=ACT.Sqrt, bias=-1.0)
 
         def sums(unit):
+            dist = dist_of[unit]
             root = root_of[unit]
-            part = part_of_dist(unit)
-            nc.gpsimd.tensor_tensor(
-                out=part[:, :, MAIN_COLS:],
-                in0=root[:, :, MAIN_COLS:],
-                in1=part[:, :, MAIN_COLS:],
-                op=ALU.subtract,
-            )
             nc.vector.tensor_tensor(
-                out=part[:, :, :MAIN_COLS],
-                in0=root[:, :, :MAIN_COLS],
-                in1=part[:, :, :MAIN_COLS],
-                op=ALU.subtract,
+                out=dist[:, :MAIN_COLS], in0=root[:, :MAIN_COLS], in1=dist[:, :MAIN_COLS], op=ALU.subtract
+            )
+            nc.gpsimd.tensor_tensor(
+                out=dist[:, MAIN_COLS:], in0=root[:, MAIN_COLS:], in1=dist[:, MAIN_COLS:], op=ALU.subtract
             )
 
-        def logs():
-            for first in range(0, ITEMS, LOG_COLS):
-                for user_tile in range(USER_TILES):
-                    piece = dist[:, user_tile, first : first + LOG_COLS]
-                    nc.scalar.activation(out=piece, in_=piece, func=ACT.Ln)
-                    nc.vector.scalar_tensor_tensor(
-                        out=piece, in0=piece, scalar=-1.0, in1=piece, op0=ALU.mult, op1=ALU.mult
-                    )
-                    nc.sync.dma_start(
-                        out=out_rows[:, user_tile, first : first + LOG_COLS], in_=piece
-                    )
+        def logs(unit):
+            m, q = divmod(unit, USER_PAIRS)
+            for j in range(UNIT_TILES):
+                piece = dist_of[unit][:, j * ROW_COLS : (j + 1) * ROW_COLS]
+                nc.scalar.activation(out=piece, in_=piece, func=ACT.Ln)
+                nc.vector.scalar_tensor_tensor(
+                    out=piece, in0=piece, scalar=-1.0, in1=piece, op0=ALU.mult, op1=ALU.mult
+                )
+                nc.sync.dma_start(
+                    out=out_rows[:, q * UNIT_TILES + j, m * ROW_COLS : (m + 1) * ROW_COLS], in_=piece
+                )
 
         with tc.manual_schedule():
             for chunk in first_chunks + later_chunks:
                 load(chunk)
+            for chunk in first_chunks:
+                flip_sign(chunk)
             for chunk in first_chunks:
                 turn(chunk)
                 quantise(chunk)
@@ -230,10 +220,11 @@ def tile_hgatmodel_kernel(tc, h, out):
                     sums(r - SUM_LAG)
                 if r < UNITS:
                     products(r)
-                for chunk in later_chunks:
-                    if chunk["first_round"] == r + QUANTISE_LEAD:
-                        quantise(chunk)
-                for chunk in later_chunks:
-                    if chunk["first_round"] == r + TURN_LEAD:
-                        turn(chunk)
-            logs()
+                if 0 <= r - 1 < len(later_chunks):
+                    quantise(later_chunks[r - 1])
+                if r < len(later_chunks):
+                    turn(later_chunks[r])
+                if r + 1 < len(later_chunks):
+                    flip_sign(later_chunks[r + 1])
+            for unit in range(UNITS):
+                logs(unit)

@@ -21,23 +21,25 @@ PACK = 4
 WORDS = DIM // 2
 USER_TILES = USERS // P
 
-CHUNK_TILES = 4
+CHUNK_TILES = 2
 CHUNK_ROWS = CHUNK_TILES * P
+USER_CHUNKS = USERS // CHUNK_ROWS
 ITEM_CHUNKS = ITEMS // CHUNK_ROWS
-BANK_TILES = 2
 
-UNIT_TILES = 2
-UNIT_CHUNKS = 2
-ROW_COLS = UNIT_CHUNKS * CHUNK_ROWS
-UNIT_COLS = UNIT_TILES * ROW_COLS
-USER_PAIRS = USER_TILES // UNIT_TILES
-UNITS = USER_PAIRS * (ITEM_CHUNKS // UNIT_CHUNKS)
-POOL_COLS = 384
-MAIN_COLS = UNIT_COLS - POOL_COLS
+PASS_COLS = 512
+ROW_COLS = 2 * PASS_COLS
+ROW_CHUNKS = ROW_COLS // CHUNK_ROWS
+UNIT_COLS = CHUNK_TILES * ROW_COLS
+UNITS = USER_CHUNKS * (ITEMS // ROW_COLS)
+POOL_SQUARE_COLS = 448
+POOL_SUM_COLS = 320
+SQUARE_COLS = UNIT_COLS - POOL_SQUARE_COLS
+SUM_COLS = UNIT_COLS - POOL_SUM_COLS
 
 SQUARE_LAG = 1
 ROOT_LAG = 2
 SUM_LAG = 4
+CHUNKS_A_ROUND = 2
 
 MIN_THETA = 1.0 + 1e-7
 MAX_SQDIST = 50.0
@@ -53,8 +55,8 @@ def tile_hgatmodel_kernel(tc, h, out):
     with ExitStack() as ctx:
         consts = ctx.enter_context(tc.tile_pool(name="consts", bufs=1))
         operands = ctx.enter_context(tc.tile_pool(name="operands", bufs=1))
-        rows_pool = ctx.enter_context(tc.tile_pool(name="rows", bufs=6))
-        grouped_pool = ctx.enter_context(tc.tile_pool(name="grouped", bufs=2))
+        rows_pool = ctx.enter_context(tc.tile_pool(name="rows", bufs=12))
+        grouped_pool = ctx.enter_context(tc.tile_pool(name="grouped", bufs=2 * CHUNKS_A_ROUND))
         dist_pool = ctx.enter_context(tc.tile_pool(name="dist", bufs=1))
         root_pool = ctx.enter_context(tc.tile_pool(name="root", bufs=4))
         turned_psum = ctx.enter_context(tc.psum_pool(name="turned", bufs=2))
@@ -91,17 +93,22 @@ def tile_hgatmodel_kernel(tc, h, out):
                 is_item=True,
             )
 
-        first_chunks = [user_chunk(0), item_chunk(0), item_chunk(1)]
-        later_chunks = [user_chunk(1)] + [item_chunk(n) for n in range(UNIT_CHUNKS, ITEM_CHUNKS)]
+        first_chunks = [user_chunk(0)] + [item_chunk(n) for n in range(ROW_CHUNKS)]
+        later_chunks = [user_chunk(q) for q in range(1, USER_CHUNKS)] + [
+            item_chunk(n) for n in range(ROW_CHUNKS, ITEM_CHUNKS)
+        ]
+
+        def later_chunks_of(step):
+            if step < 0:
+                return []
+            return later_chunks[step * CHUNKS_A_ROUND : (step + 1) * CHUNKS_A_ROUND]
 
         dist_of = {}
         root_of = {}
 
         def load(chunk):
             rows = rows_pool.tile([P, CHUNK_TILES, DIM], BF16)
-            for first in range(0, CHUNK_TILES, BANK_TILES):
-                tiles = slice(first, first + BANK_TILES)
-                nc.sync.dma_start(out=rows[:, tiles, :], in_=chunk["source"][:, tiles, :])
+            nc.sync.dma_start(out=rows[:], in_=chunk["source"])
             chunk["rows"] = rows
 
         def flip_sign(chunk):
@@ -113,24 +120,17 @@ def tile_hgatmodel_kernel(tc, h, out):
             rows = chunk["rows"]
             words = rows[:].rearrange("p t d -> p (t d)").bitcast(F32)
             grouped = grouped_pool.tile([P, CHUNK_ROWS * PACK], BF16, align_bytes=64)
-            grouped_words = grouped[:].bitcast(F32)
-            bank_words = BANK_TILES * WORDS
-            for b in range(CHUNK_TILES // BANK_TILES):
-                turned = turned_psum.tile([P, BANK_TILES, 2, P], F32)
-                for a in range(BANK_TILES):
-                    for u in range(2):
-                        first = (b * BANK_TILES + a) * WORDS + u * P
-                        nc.tensor.transpose(
-                            out=turned[:, a, u, :],
-                            in_=words[:, first : first + P],
-                            identity=identity[:],
-                        )
-                nc.scalar.copy(
-                    out=grouped_words[:, b * bank_words : (b + 1) * bank_words].rearrange(
-                        "p (a r u) -> p a r u", a=BANK_TILES, u=2
-                    ),
-                    in_=turned[:].rearrange("p a u r -> p a r u"),
-                )
+            turned = turned_psum.tile([P, CHUNK_TILES, 2, P], F32)
+            for a in range(CHUNK_TILES):
+                for u in range(2):
+                    first = a * WORDS + u * P
+                    nc.tensor.transpose(
+                        out=turned[:, a, u, :], in_=words[:, first : first + P], identity=identity[:]
+                    )
+            nc.scalar.copy(
+                out=grouped[:].bitcast(F32).rearrange("p (a r u) -> p a r u", a=CHUNK_TILES, u=2),
+                in_=turned[:].rearrange("p a u r -> p a r u"),
+            )
             chunk["grouped"] = grouped
 
         def quantise(chunk):
@@ -141,25 +141,25 @@ def tile_hgatmodel_kernel(tc, h, out):
             )
 
         def products(unit):
-            m, q = divmod(unit, USER_PAIRS)
+            m, q = divmod(unit, USER_CHUNKS)
             dist = dist_pool.tile([P, UNIT_COLS], F32, name="dist%d" % unit)
-            for j in range(UNIT_TILES):
-                user_first = (q * UNIT_TILES + j) * P
-                for c in range(UNIT_CHUNKS):
-                    item_first = (m * UNIT_CHUNKS + c) * CHUNK_ROWS
-                    prod = prod_psum.tile([P, CHUNK_ROWS], F32)
+            for j in range(CHUNK_TILES):
+                user_first = (q * CHUNK_TILES + j) * P
+                for within_row in range(0, ROW_COLS, PASS_COLS):
+                    item_first = m * ROW_COLS + within_row
+                    prod = prod_psum.tile([P, PASS_COLS], F32)
                     nc.tensor.matmul_mx(
                         out=prod[:],
                         lhsT=user_codes[:, user_first : user_first + P].bitcast(FP8X4),
                         lhsT_scale=user_scales[:, user_first : user_first + P],
-                        rhs=item_codes[:, item_first : item_first + CHUNK_ROWS].bitcast(FP8X4),
-                        rhs_scale=item_scales[:, item_first : item_first + CHUNK_ROWS],
+                        rhs=item_codes[:, item_first : item_first + PASS_COLS].bitcast(FP8X4),
+                        rhs_scale=item_scales[:, item_first : item_first + PASS_COLS],
                         start=True,
                         stop=True,
                     )
-                    dist_first = j * ROW_COLS + c * CHUNK_ROWS
+                    dist_first = j * ROW_COLS + within_row
                     nc.vector.tensor_scalar(
-                        out=dist[:, dist_first : dist_first + CHUNK_ROWS],
+                        out=dist[:, dist_first : dist_first + PASS_COLS],
                         in0=prod[:],
                         scalar1=-MIN_THETA,
                         scalar2=-MAX_THETA,
@@ -171,9 +171,14 @@ def tile_hgatmodel_kernel(tc, h, out):
         def squares(unit):
             dist = dist_of[unit]
             root = root_pool.tile([P, UNIT_COLS], F32)
-            nc.scalar.activation(out=root[:, :MAIN_COLS], in_=dist[:, :MAIN_COLS], func=ACT.Square)
+            nc.scalar.activation(
+                out=root[:, :SQUARE_COLS], in_=dist[:, :SQUARE_COLS], func=ACT.Square
+            )
             nc.gpsimd.tensor_tensor(
-                out=root[:, MAIN_COLS:], in0=dist[:, MAIN_COLS:], in1=dist[:, MAIN_COLS:], op=ALU.mult
+                out=root[:, SQUARE_COLS:],
+                in0=dist[:, SQUARE_COLS:],
+                in1=dist[:, SQUARE_COLS:],
+                op=ALU.mult,
             )
             root_of[unit] = root
 
@@ -185,22 +190,22 @@ def tile_hgatmodel_kernel(tc, h, out):
             dist = dist_of[unit]
             root = root_of[unit]
             nc.vector.tensor_tensor(
-                out=dist[:, :MAIN_COLS], in0=root[:, :MAIN_COLS], in1=dist[:, :MAIN_COLS], op=ALU.subtract
+                out=dist[:, :SUM_COLS], in0=root[:, :SUM_COLS], in1=dist[:, :SUM_COLS], op=ALU.subtract
             )
             nc.gpsimd.tensor_tensor(
-                out=dist[:, MAIN_COLS:], in0=root[:, MAIN_COLS:], in1=dist[:, MAIN_COLS:], op=ALU.subtract
+                out=dist[:, SUM_COLS:], in0=root[:, SUM_COLS:], in1=dist[:, SUM_COLS:], op=ALU.subtract
             )
 
         def logs(unit):
-            m, q = divmod(unit, USER_PAIRS)
-            for j in range(UNIT_TILES):
+            m, q = divmod(unit, USER_CHUNKS)
+            for j in range(CHUNK_TILES):
                 piece = dist_of[unit][:, j * ROW_COLS : (j + 1) * ROW_COLS]
                 nc.scalar.activation(out=piece, in_=piece, func=ACT.Ln)
                 nc.vector.scalar_tensor_tensor(
                     out=piece, in0=piece, scalar=-1.0, in1=piece, op0=ALU.mult, op1=ALU.mult
                 )
                 nc.sync.dma_start(
-                    out=out_rows[:, q * UNIT_TILES + j, m * ROW_COLS : (m + 1) * ROW_COLS], in_=piece
+                    out=out_rows[:, q * CHUNK_TILES + j, m * ROW_COLS : (m + 1) * ROW_COLS], in_=piece
                 )
 
         with tc.manual_schedule():
@@ -211,20 +216,20 @@ def tile_hgatmodel_kernel(tc, h, out):
             for chunk in first_chunks:
                 turn(chunk)
                 quantise(chunk)
-            for r in range(UNITS + SUM_LAG):
+            for r in range(-1, UNITS + SUM_LAG):
                 if 0 <= r - SQUARE_LAG < UNITS:
                     squares(r - SQUARE_LAG)
                 if 0 <= r - ROOT_LAG < UNITS:
                     roots(r - ROOT_LAG)
                 if 0 <= r - SUM_LAG:
                     sums(r - SUM_LAG)
-                if r < UNITS:
+                if 0 <= r < UNITS:
                     products(r)
-                if 0 <= r - 1 < len(later_chunks):
-                    quantise(later_chunks[r - 1])
-                if r < len(later_chunks):
-                    turn(later_chunks[r])
-                if r + 1 < len(later_chunks):
-                    flip_sign(later_chunks[r + 1])
+                for chunk in later_chunks_of(r):
+                    quantise(chunk)
+                for chunk in later_chunks_of(r + 1):
+                    turn(chunk)
+                for chunk in later_chunks_of(r + 2):
+                    flip_sign(chunk)
             for unit in range(UNITS):
                 logs(unit)

@@ -31,8 +31,8 @@ ROW_COLS = 2 * PASS_COLS
 ROW_CHUNKS = ROW_COLS // CHUNK_ROWS
 UNIT_COLS = CHUNK_TILES * ROW_COLS
 UNITS = USER_CHUNKS * (ITEMS // ROW_COLS)
-POOL_SQUARE_COLS = 448
-POOL_SUM_COLS = 320
+POOL_SQUARE_COLS = 512
+POOL_SUM_COLS = 384
 SQUARE_COLS = UNIT_COLS - POOL_SQUARE_COLS
 SUM_COLS = UNIT_COLS - POOL_SUM_COLS
 

from contextlib import ExitStack

import concourse.mybir as mybir
from concourse.masks import make_identity

F32 = mybir.dt.float32
BF16 = mybir.dt.bfloat16
U32 = mybir.dt.uint32
U8 = mybir.dt.uint8
FP8X4 = mybir.dt.float8_e4m3fn_x4
ALU = mybir.AluOpType
ACT = mybir.ActivationFunctionType

P = 128
USERS = 1024
ITEMS = 4096
DIM = 512
FLOPS = 2 * USERS * ITEMS * DIM

PACK = 4
WORDS = DIM // 2
USER_TILES = USERS // P

CHUNK_TILES = 2
CHUNK_ROWS = CHUNK_TILES * P
USER_CHUNKS = USERS // CHUNK_ROWS
ITEM_CHUNKS = ITEMS // CHUNK_ROWS

PASS_COLS = 512
ROW_COLS = 2 * PASS_COLS
ROW_CHUNKS = ROW_COLS // CHUNK_ROWS
UNIT_COLS = CHUNK_TILES * ROW_COLS
UNITS = USER_CHUNKS * (ITEMS // ROW_COLS)
POOL_SQUARE_COLS = 512
POOL_SUM_COLS = 384
SQUARE_COLS = UNIT_COLS - POOL_SQUARE_COLS
SUM_COLS = UNIT_COLS - POOL_SUM_COLS

SQUARE_LAG = 1
ROOT_LAG = 2
SUM_LAG = 4
CHUNKS_A_ROUND = 2

MIN_THETA = 1.0 + 1e-7
MAX_SQDIST = 50.0
EULER = 2.718281828459045
MAX_THETA = 0.5 * (EULER ** (MAX_SQDIST**0.5) + EULER ** -(MAX_SQDIST**0.5))


def tile_hgatmodel_kernel(tc, h, out):
    nc = tc.nc
    users = h[0:USERS, :].rearrange("(p t) d -> p t d", t=USER_TILES)
    out_rows = out.rearrange("(p t) i -> p t i", t=USER_TILES)

    with ExitStack() as ctx:
        consts = ctx.enter_context(tc.tile_pool(name="consts", bufs=1))
        operands = ctx.enter_context(tc.tile_pool(name="operands", bufs=1))
        rows_pool = ctx.enter_context(tc.tile_pool(name="rows", bufs=12))
        grouped_pool = ctx.enter_context(tc.tile_pool(name="grouped", bufs=2 * CHUNKS_A_ROUND))
        dist_pool = ctx.enter_context(tc.tile_pool(name="dist", bufs=1))
        root_pool = ctx.enter_context(tc.tile_pool(name="root", bufs=4))
        turned_psum = ctx.enter_context(tc.psum_pool(name="turned", bufs=2))
        prod_psum = ctx.enter_context(tc.psum_pool(name="prod", bufs=6))

        identity = consts.tile([P, P], F32)
        make_identity(nc, identity[:])
        one = consts.tile([P, 1], F32)
        nc.vector.memset(one[:], 1.0)
        warm = consts.tile([P, 1], F32)
        nc.scalar.activation(out=warm[:], in_=one[:], func=ACT.Sqrt)

        user_codes = operands.tile([P, USERS], U32, align_bytes=64)
        user_scales = operands.tile([P, USERS], U8, align_bytes=64)
        item_codes = operands.tile([P, ITEMS], U32, align_bytes=64)
        item_scales = operands.tile([P, ITEMS], U8, align_bytes=64)

        def user_chunk(g):
            cols = slice(g * CHUNK_ROWS, (g + 1) * CHUNK_ROWS)
            return dict(
                source=users[:, g * CHUNK_TILES : (g + 1) * CHUNK_TILES, :],
                codes=user_codes[:, cols],
                scales=user_scales[:, cols],
                is_item=False,
            )

        def item_chunk(n):
            cols = slice(n * CHUNK_ROWS, (n + 1) * CHUNK_ROWS)
            first = USERS + n * CHUNK_ROWS
            return dict(
                source=h[first : first + CHUNK_ROWS, :].rearrange("(t p) d -> p t d", p=P),
                codes=item_codes[:, cols],
                scales=item_scales[:, cols],
                is_item=True,
            )

        first_chunks = [user_chunk(0)] + [item_chunk(n) for n in range(ROW_CHUNKS)]
        later_chunks = [user_chunk(q) for q in range(1, USER_CHUNKS)] + [
            item_chunk(n) for n in range(ROW_CHUNKS, ITEM_CHUNKS)
        ]

        def later_chunks_of(step):
            if step < 0:
                return []
            return later_chunks[step * CHUNKS_A_ROUND : (step + 1) * CHUNKS_A_ROUND]

        dist_of = {}
        root_of = {}

        def load(chunk):
            rows = rows_pool.tile([P, CHUNK_TILES, DIM], BF16)
            nc.sync.dma_start(out=rows[:], in_=chunk["source"])
            chunk["rows"] = rows

        def flip_sign(chunk):
            if chunk["is_item"]:
                first_coordinate = chunk["rows"][:, :, 0:1]
                nc.vector.tensor_scalar_mul(out=first_coordinate, in0=first_coordinate, scalar1=-1.0)

        def turn(chunk):
            rows = chunk["rows"]
            words = rows[:].rearrange("p t d -> p (t d)").bitcast(F32)
            grouped = grouped_pool.tile([P, CHUNK_ROWS * PACK], BF16, align_bytes=64)
            turned = turned_psum.tile([P, CHUNK_TILES, 2, P], F32)
            for a in range(CHUNK_TILES):
                for u in range(2):
                    first = a * WORDS + u * P
                    nc.tensor.transpose(
                        out=turned[:, a, u, :], in_=words[:, first : first + P], identity=identity[:]
                    )
            nc.scalar.copy(
                out=grouped[:].bitcast(F32).rearrange("p (a r u) -> p a r u", a=CHUNK_TILES, u=2),
                in_=turned[:].rearrange("p a u r -> p a r u"),
            )
            chunk["grouped"] = grouped

        def quantise(chunk):
            nc.vector.quantize_mx(
                out=chunk["codes"].bitcast(FP8X4),
                scales=chunk["scales"],
                in_=chunk["grouped"][:],
            )

        def products(unit):
            m, q = divmod(unit, USER_CHUNKS)
            dist = dist_pool.tile([P, UNIT_COLS], F32, name="dist%d" % unit)
            for j in range(CHUNK_TILES):
                user_first = (q * CHUNK_TILES + j) * P
                for within_row in range(0, ROW_COLS, PASS_COLS):
                    item_first = m * ROW_COLS + within_row
                    prod = prod_psum.tile([P, PASS_COLS], F32)
                    nc.tensor.matmul_mx(
                        out=prod[:],
                        lhsT=user_codes[:, user_first : user_first + P].bitcast(FP8X4),
                        lhsT_scale=user_scales[:, user_first : user_first + P],
                        rhs=item_codes[:, item_first : item_first + PASS_COLS].bitcast(FP8X4),
                        rhs_scale=item_scales[:, item_first : item_first + PASS_COLS],
                        start=True,
                        stop=True,
                    )
                    dist_first = j * ROW_COLS + within_row
                    nc.vector.tensor_scalar(
                        out=dist[:, dist_first : dist_first + PASS_COLS],
                        in0=prod[:],
                        scalar1=-MIN_THETA,
                        scalar2=-MAX_THETA,
                        op0=ALU.min,
                        op1=ALU.max,
                    )
            dist_of[unit] = dist

        def squares(unit):
            dist = dist_of[unit]
            root = root_pool.tile([P, UNIT_COLS], F32)
            nc.scalar.activation(
                out=root[:, :SQUARE_COLS], in_=dist[:, :SQUARE_COLS], func=ACT.Square
            )
            nc.gpsimd.tensor_tensor(
                out=root[:, SQUARE_COLS:],
                in0=dist[:, SQUARE_COLS:],
                in1=dist[:, SQUARE_COLS:],
                op=ALU.mult,
            )
            root_of[unit] = root

        def roots(unit):
            root = root_of[unit]
            nc.scalar.activation(out=root[:], in_=root[:], func=ACT.Sqrt, bias=-1.0)

        def sums(unit):
            dist = dist_of[unit]
            root = root_of[unit]
            nc.vector.tensor_tensor(
                out=dist[:, :SUM_COLS], in0=root[:, :SUM_COLS], in1=dist[:, :SUM_COLS], op=ALU.subtract
            )
            nc.gpsimd.tensor_tensor(
                out=dist[:, SUM_COLS:], in0=root[:, SUM_COLS:], in1=dist[:, SUM_COLS:], op=ALU.subtract
            )

        def logs(unit):
            m, q = divmod(unit, USER_CHUNKS)
            for j in range(CHUNK_TILES):
                piece = dist_of[unit][:, j * ROW_COLS : (j + 1) * ROW_COLS]
                nc.scalar.activation(out=piece, in_=piece, func=ACT.Ln)
                nc.vector.scalar_tensor_tensor(
                    out=piece, in0=piece, scalar=-1.0, in1=piece, op0=ALU.mult, op1=ALU.mult
                )
                nc.sync.dma_start(
                    out=out_rows[:, q * CHUNK_TILES + j, m * ROW_COLS : (m + 1) * ROW_COLS], in_=piece
                )

        with tc.manual_schedule():
            for chunk in first_chunks + later_chunks:
                load(chunk)
            for chunk in first_chunks:
                flip_sign(chunk)
            for chunk in first_chunks:
                turn(chunk)
                quantise(chunk)
            for r in range(-1, UNITS + SUM_LAG):
                if 0 <= r - SQUARE_LAG < UNITS:
                    squares(r - SQUARE_LAG)
                if 0 <= r - ROOT_LAG < UNITS:
                    roots(r - ROOT_LAG)
                if 0 <= r - SUM_LAG:
                    sums(r - SUM_LAG)
                if 0 <= r < UNITS:
                    products(r)
                for chunk in later_chunks_of(r):
                    quantise(chunk)
                for chunk in later_chunks_of(r + 1):
                    turn(chunk)
                for chunk in later_chunks_of(r + 2):
                    flip_sign(chunk)
            for unit in range(UNITS):
                logs(unit)
